import numpy as np
import ml_dtypes


def mxq(x, axis, fmt="e4m3"):
    dtype, down = {"e4m3": (ml_dtypes.float8_e4m3fn, 7), "e5m2": (ml_dtypes.float8_e5m2, 14)}[fmt]
    v = np.moveaxis(np.asarray(x, np.float32).astype(ml_dtypes.bfloat16).astype(np.float64), axis, -1)
    blocks = v.reshape(v.shape[:-1] + (-1, 32))
    amax = np.abs(blocks).max(-1, keepdims=True)
    byte = np.maximum(np.where(amax > 0, np.frexp(amax)[1] - 1 + 127, 0) - down, 1)
    scale = np.exp2(byte - 127.0)
    codes = (blocks / scale).astype(np.float32).astype(dtype).astype(np.float64)
    return np.moveaxis((codes * scale).reshape(v.shape), -1, axis)


WIDE = False


def mx_kscale(k):
    if not WIDE:
        return np.ones(k)
    levels = np.array([10, -10, 5, -5, 0])
    if k % 512:
        return np.exp2(np.random.permutation(np.resize(levels, k // 32))).repeat(32)
    a = np.empty((k // 512, 16))
    for p in range(k // 512):
        a[p, :8] = np.random.permutation(np.resize(levels, 8))
        for g in range(8):
            far = levels[np.abs(levels - a[p, g]) >= 10]
            a[p, g + 8] = far[np.random.randint(len(far))]
    return np.exp2(a.ravel()).repeat(32)


BF16 = ml_dtypes.bfloat16


def bf(x):
    return np.asarray(x, np.float32).astype(BF16)


def f64(x):
    return np.asarray(x).astype(np.float64)


B, N, D, H, DH = 4, 640, 1024, 16, 64
R = 2 * DH
EPS = 1e-12
BASE = 10000.0


def l2norm(t):
    n = np.sqrt(np.sum(t * t, axis=-1, keepdims=True))
    return t / np.maximum(n, EPS)


def rotate_half(t):
    t1, t2 = np.split(t, 2, axis=-1)
    return np.concatenate([-t2, t1], axis=-1)


def rope_tables():
    inv_freq = 1.0 / (BASE ** (np.arange(0, R, 2) / R))
    freqs = np.outer(np.arange(N), inv_freq)
    emb = np.concatenate([freqs, freqs], axis=-1)
    return np.cos(emb), np.sin(emb)


def draw0():
    s, t = mx_kscale(D), mx_kscale(D)
    g = 0.5 * np.sqrt(DH)
    return {
        "x": bf(np.random.standard_normal((B, N, D)) * s),
        "a": bf(np.random.standard_normal((B, N, D)) * t),
        "Wq_x": bf(np.random.standard_normal((H * DH, D)) / np.sqrt(D) / s),
        "Wq_a": bf(np.random.standard_normal((H * DH, D)) / np.sqrt(D) / t),
        "qx_scale": bf(g * (1.0 + 0.1 * np.random.standard_normal((H, 1, DH)))),
        "qa_scale": bf(g * (1.0 + 0.1 * np.random.standard_normal((H, 1, DH)))),
    }


def core(x, a, Wq_x, Wq_a, qx_scale, qa_scale):
    q_x = mxq(f64(x), 2, "e4m3") @ mxq(f64(Wq_x), 1, "e4m3").T
    q_a = mxq(f64(a), 2, "e4m3") @ mxq(f64(Wq_a), 1, "e4m3").T
    q_x = q_x.reshape(B, N, H, DH).transpose(0, 2, 1, 3)
    q_a = q_a.reshape(B, N, H, DH).transpose(0, 2, 1, 3)
    q_x = l2norm(q_x) * f64(qx_scale)
    q_a = l2norm(q_a) * f64(qa_scale)
    q = np.concatenate([q_x, q_a], axis=-1)
    cos, sin = rope_tables()
    return q * cos + rotate_half(q) * sin


def e4m3fn_bytes(y):
    return np.clip(np.asarray(y, np.float64), -448.0, 448.0).astype(np.float32).astype(ml_dtypes.float8_e4m3fn).view(np.uint8)


def e4m3fn_values(b):
    return np.asarray(b, np.uint8).view(ml_dtypes.float8_e4m3fn).astype(np.float64)


def setup_inputs():
    d = draw0()
    x0 = np.asarray(d['x']).astype(np.float64)
    s = (np.max(np.abs(x0), axis=(0, 1), keepdims=True) / 448.0).astype(np.float32)
    out = {}
    for k, v in d.items():
        if k == 'x':
            out['x_bytes'] = e4m3fn_bytes(x0 / s.astype(np.float64))
            out['x_scale'] = s
        else:
            out[k] = v
    return out


def reference(x_bytes, x_scale, a, Wq_x, Wq_a, qx_scale, qa_scale):
    return core(e4m3fn_values(x_bytes) * x_scale.astype(np.float64), a, Wq_x, Wq_a, qx_scale, qa_scale)

@@ -1,0 +1,334 @@
+from contextlib import ExitStack
+
+import concourse.mybir as mybir
+from concourse.masks import make_identity
+
+F32 = mybir.dt.float32
+BF16 = mybir.dt.bfloat16
+U32 = mybir.dt.uint32
+U8 = mybir.dt.uint8
+I32 = mybir.dt.int32
+FP8 = mybir.dt.float8_e4m3fn
+FP8X4 = mybir.dt.float8_e4m3fn_x4
+ALU = mybir.AluOpType
+ACT = mybir.ActivationFunctionType
+
+B, N, D, H, DH = 4, 640, 1024, 16, 64
+P = 128
+NBLK = N // P
+NPASS = D // 512
+HGRP = 8
+NT = B * NBLK
+NQ = 2 * NT
+XD = 3
+FLOPS = 2 * 2 * B * N * D * H * DH
+
+TWO_PI = 6.283185307179586
+C1 = 6.28125
+C2 = TWO_PI - C1
+
+
+def tile_cmattention_pa_kernel(tc, x_bytes, x_scale, a, Wq_x, Wq_a, qx_scale, qa_scale, out):
+    nc = tc.nc
+    with ExitStack() as ctx:
+        const = ctx.enter_context(tc.tile_pool(name="const", bufs=1))
+        ldpool = ctx.enter_context(tc.tile_pool(name="ldpool", bufs=2))
+        prep = ctx.enter_context(tc.tile_pool(name="prep", bufs=2))
+        tabs = ctx.enter_context(tc.tile_pool(name="tabs", bufs=2))
+        tp = ctx.enter_context(tc.psum_pool(name="tp", bufs=2))
+        mm = ctx.enter_context(tc.psum_pool(name="mm", bufs=6))
+
+        W_in = (Wq_x, Wq_a)
+        tiles = [(blk, b) for blk in range(NBLK) for b in range(B)]
+        x8s = {}
+        a_sbs = {}
+        xbfs = {}
+        groupeds = {}
+        codes = {}
+        banks = {}
+        rs = {}
+        T = {}
+
+        def load_blk(blk):
+            xt = ldpool.tile([P, B, D], U8, name="x8", tag="x8")
+            nc.sync.dma_start(out=xt[:], in_=x_bytes[:, blk * P:(blk + 1) * P, :].rearrange("b p k -> p b k"))
+            x8s[blk] = xt
+            at = ldpool.tile([P, B, D], BF16, name="a_sb", tag="a_sb")
+            nc.sync.dma_start(out=at[:], in_=a[:, blk * P:(blk + 1) * P, :].rearrange("b p k -> p b k"))
+            a_sbs[blk] = at
+
+        ident = const.tile([P, P], F32, name="ident")
+        make_identity(nc, ident[:])
+        tiny = const.tile([P, 1], F32, name="tiny")
+        nc.vector.memset(tiny[:], 1e-24)
+        negtiny = const.tile([P, 1], F32, name="negtiny")
+        nc.vector.memset(negtiny[:], -1e-24)
+        xs_bc = const.tile([P, D], F32, name="xs_bc")
+        cs = [const.tile([P, NBLK, 2, DH], F32, name="cs%d" % tab) for tab in range(2)]
+        csT = const.tile([P, 2 * NBLK, P], F32, name="csT")
+        gcol = const.tile([P, 2 * H], F32, name="gcol")
+        Bm = [const.tile([P, H, P], F32, name="Bm%d" % tab) for tab in range(2)]
+        wcodes = [const.tile([P, NPASS, H * DH], U32, name="wcodes%d" % s, align_bytes=64) for s in range(2)]
+        wscl = [const.tile([P, NPASS, H * DH], U8, name="wscl%d" % s, align_bytes=64) for s in range(2)]
+
+        def transpose_rows(bank, words):
+            for g in range(NPASS):
+                for u in range(2):
+                    nc.tensor.transpose(bank[:, g, u, :], words[:, 256 * g + u:256 * (g + 1):2], ident[:])
+
+        def table_piece(blk, i):
+            tab = i // 4
+            h0 = 4 * (i % 4)
+            if (blk, tab) not in T:
+                T[(blk, tab)] = tabs.tile([P, H, 2, DH], F32, name="T%d" % tab, tag="T%d" % tab)
+            bank = tp.tile([P, 512], F32, name="tpbank", tag="tpbank")
+            nc.tensor.matmul(out=bank[:], lhsT=csT[:, 2 * blk + tab, :],
+                             rhs=Bm[tab][:, h0:h0 + 4, :].rearrange("p h c -> p (h c)"), start=True, stop=True)
+            nc.scalar.copy(out=T[(blk, tab)][:, h0:h0 + 4, :, :].rearrange("p h e j -> p (h e j)"), in_=bank[:])
+
+        def widen(t):
+            blk, b = tiles[t]
+            xbf = prep.tile([P, D], BF16, name="xbf", tag="xbf", bufs=XD + 2)
+            nc.vector.tensor_tensor(out=xbf[:], in0=x8s[blk][:, b, :].bitcast(FP8), in1=xs_bc[:], op=ALU.mult)
+            xbfs[t] = xbf
+
+        def turn(t):
+            blk, b = tiles[t]
+            grouped = prep.tile([P, 2, NPASS, P, 4], BF16, name="grouped", tag="grouped", align_bytes=64)
+            srcs = (xbfs[t][:].bitcast(F32), a_sbs[blk][:, b, :].bitcast(F32))
+            for s in range(2):
+                bank = tp.tile([P, NPASS, 2, P], F32, name="tpbank", tag="tpbank")
+                transpose_rows(bank, srcs[s])
+                nc.scalar.copy(out=grouped[:, s, :, :, :].bitcast(F32), in_=bank[:].rearrange("p g u r -> p g r u"))
+            groupeds[t] = grouped
+            if t % B == B - 1 and t // B + 2 < NBLK:
+                load_blk(t // B + 2)
+
+        def quantise(t):
+            cd = prep.tile([P, 2, NPASS, P], U32, name="codes", tag="codes", bufs=3, align_bytes=64)
+            sc = prep.tile([P, 2, NPASS, P], U8, name="scl", tag="scl", bufs=3, align_bytes=64)
+            nc.vector.quantize_mx(
+                out=cd[:].rearrange("p s g r -> p (s g r)").bitcast(FP8X4),
+                scales=sc[:].rearrange("p s g r -> p (s g r)"),
+                in_=groupeds[t][:].rearrange("p s g r j -> p (s g r j)"),
+            )
+            codes[t] = (cd, sc)
+
+        def matmuls(q):
+            t, hg = q // 2, q % 2
+            cd, sc = codes[t]
+            pair = []
+            for s in range(2):
+                ps = mm.tile([P, 512], F32, name="mmbank", tag="mmbank")
+                for g in range(NPASS):
+                    nc.tensor.matmul_mx(
+                        out=ps[:],
+                        lhsT=cd[:, s, g, :].bitcast(FP8X4),
+                        lhsT_scale=sc[:, s, g, :],
+                        rhs=wcodes[s][:, g, hg * 512:(hg + 1) * 512].bitcast(FP8X4),
+                        rhs_scale=wscl[s][:, g, hg * 512:(hg + 1) * 512],
+                        start=(g == 0),
+                        stop=(g == NPASS - 1),
+                    )
+                pair.append(ps)
+            banks[q] = pair
+
+        def prep_steps(q):
+            if 0 <= q // 2 + 2 < NT:
+                quantise(q // 2 + 2)
+            if 0 <= q // 2 + 3 + XD < NT:
+                widen(q // 2 + 3 + XD)
+
+        with tc.tile_pool(name="head", bufs=1) as head:
+            graw = head.tile([P, P], BF16, name="graw")
+            nc.vector.memset(graw[:], 0.0)
+            for s in range(2):
+                for e in range(2):
+                    nc.sync.dma_start(out=graw[s * H:(s + 1) * H, e * DH:(e + 1) * DH],
+                                      in_=(qx_scale, qa_scale)[s].rearrange("h o j -> h (o j)"))
+            wraw = {}
+
+            def load_w(s, half):
+                t = head.tile([P, 4, D], BF16, name="wraw%d%d" % (s, half))
+                for c in range(2):
+                    nc.sync.dma_start(
+                        out=t[:, 2 * c:2 * c + 2, :],
+                        in_=W_in[s][half * 512 + c * 256:half * 512 + (c + 1) * 256, :].rearrange("(r p) k -> p r k", p=P),
+                    )
+                wraw[(s, half)] = t
+
+            load_w(0, 0)
+            load_w(1, 0)
+            gbc = []
+            for s in range(2):
+                gb = head.tile([P, H, DH], BF16, name="gbc%d" % s)
+                nc.sync.dma_start(out=gb[:].rearrange("p h j -> p (h j)"),
+                                  in_=(qx_scale, qa_scale)[s].rearrange("h o j -> (h o j)").partition_broadcast(P))
+                gbc.append(gb)
+            nc.sync.dma_start(out=xs_bc[:], in_=x_scale.rearrange("o q k -> (o q k)").partition_broadcast(P))
+            load_blk(0)
+            load_w(0, 1)
+            load_w(1, 1)
+            load_blk(1)
+
+            gf = head.tile([P, P], F32, name="gf")
+            nc.vector.tensor_copy(out=gf[:], in_=graw[:])
+            gbank = tp.tile([P, 512], F32, name="tpbank", tag="tpbank")
+            nc.tensor.transpose(gbank[:, 0:P], gf[:], ident[:])
+            nc.scalar.copy(out=gcol[:], in_=gbank[:, 0:2 * H])
+
+            freq = head.tile([P, DH], F32, name="freq")
+            nc.vector.memset(freq[:], 1.0)
+            for bit in range(6):
+                c = 2 ** bit
+                view = freq[:].rearrange("p (a two c) -> p a two c", two=2, c=c)[:, :, 1, :]
+                nc.vector.tensor_scalar_mul(out=view, in0=view, scalar1=10000.0 ** (-c / 64.0))
+            n_i = head.tile([P, NBLK], I32, name="n_i")
+            nc.gpsimd.iota(n_i[:], pattern=[[P, NBLK]], base=0, channel_multiplier=1)
+            n_f = head.tile([P, NBLK], F32, name="n_f")
+            nc.vector.tensor_copy(out=n_f[:], in_=n_i[:])
+            theta = head.tile([P, NBLK, DH], F32, name="theta")
+            nc.vector.tensor_tensor(out=theta[:], in0=freq[:].unsqueeze(1).to_broadcast([P, NBLK, DH]),
+                                    in1=n_f[:].unsqueeze(2).to_broadcast([P, NBLK, DH]), op=ALU.mult)
+            turns = head.tile([P, NBLK, DH], F32, name="turns")
+            nc.vector.tensor_scalar(out=turns[:], in0=theta[:], scalar1=1.0 / TWO_PI, scalar2=0.25,
+                                    op0=ALU.mult, op1=ALU.add)
+            k_i = head.tile([P, NBLK, DH], I32, name="k_i")
+            nc.vector.tensor_copy(out=k_i[:], in_=turns[:])
+            k_f = head.tile([P, NBLK, DH], F32, name="k_f")
+            nc.vector.tensor_copy(out=k_f[:], in_=k_i[:])
+            red1 = head.tile([P, NBLK, DH], F32, name="red1")
+            nc.vector.scalar_tensor_tensor(out=red1[:], in0=k_f[:], scalar=-C1, in1=theta[:],
+                                           op0=ALU.mult, op1=ALU.add)
+            red = head.tile([P, NBLK, DH], F32, name="red")
+            nc.vector.scalar_tensor_tensor(out=red[:], in0=k_f[:], scalar=-C2, in1=red1[:],
+                                           op0=ALU.mult, op1=ALU.add)
+            s2 = head.tile([P, NBLK, DH], F32, name="s2")
+            nc.scalar.activation(out=s2[:], in_=red[:], func=ACT.Sin, scale=0.5)
+            s4 = head.tile([P, NBLK, DH], F32, name="s4")
+            nc.scalar.activation(out=s4[:], in_=red[:], func=ACT.Sin, scale=0.25)
+            q2 = head.tile([P, NBLK, DH], F32, name="q2")
+            nc.vector.tensor_tensor(out=q2[:], in0=s2[:], in1=s2[:], op=ALU.mult)
+            nc.vector.tensor_scalar(out=cs[0][:, :, 0, :], in0=q2[:], scalar1=-2.0, scalar2=1.0,
+                                    op0=ALU.mult, op1=ALU.add)
+            nc.vector.tensor_scalar(out=cs[1][:, :, 1, :], in0=q2[:], scalar1=-2.0, scalar2=1.0,
+                                    op0=ALU.mult, op1=ALU.add)
+            q4 = head.tile([P, NBLK, DH], F32, name="q4")
+            nc.vector.tensor_tensor(out=q4[:], in0=s4[:], in1=s4[:], op=ALU.mult)
+            c2 = head.tile([P, NBLK, DH], F32, name="c2")
+            nc.vector.tensor_scalar(out=c2[:], in0=q4[:], scalar1=-2.0, scalar2=1.0, op0=ALU.mult, op1=ALU.add)
+            nc.vector.scalar_tensor_tensor(out=cs[0][:, :, 1, :], in0=s2[:], scalar=2.0, in1=c2[:],
+                                           op0=ALU.mult, op1=ALU.mult)
+            nc.vector.scalar_tensor_tensor(out=cs[1][:, :, 0, :], in0=s2[:], scalar=-2.0, in1=c2[:],
+                                           op0=ALU.mult, op1=ALU.mult)
+
+            for tab in range(2):
+                T[(0, tab)] = tabs.tile([P, H, 2, DH], F32, name="T%d" % tab, tag="T%d" % tab)
+            for h0 in (0, HGRP):
+                for tab in range(2):
+                    nc.vector.tensor_tensor(
+                        out=T[(0, tab)][:, h0:h0 + HGRP, :, :],
+                        in0=gbc[tab][:, h0:h0 + HGRP, :].unsqueeze(2).to_broadcast([P, HGRP, 2, DH]),
+                        in1=cs[tab][:, 0, :, :].unsqueeze(1).to_broadcast([P, HGRP, 2, DH]),
+                        op=ALU.mult,
+                    )
+
+            for h in range(H):
+                for tab in range(2):
+                    nc.scalar.activation(out=Bm[tab][:, h, :], in_=ident[:], func=ACT.Copy,
+                                         scale=gcol[:, tab * H + h:tab * H + h + 1])
+
+            for half in range(2):
+                for s in range(2):
+                    gww = head.tile([P, NPASS, 512, 4], BF16, name="gww", tag="gww", bufs=2, align_bytes=64)
+                    for rr in range(4):
+                        bank = mm.tile([P, NPASS, 2, P], F32, name="mmbank", tag="mmbank")
+                        transpose_rows(bank, wraw[(s, half)][:, rr, :].bitcast(F32))
+                        dst = gww[:, :, rr * P:(rr + 1) * P, :].bitcast(F32)
+                        src = bank[:].rearrange("p g u r -> p g r u")
+                        if rr % 2 == 0:
+                            nc.vector.tensor_copy(out=dst, in_=src)
+                        else:
+                            nc.scalar.copy(out=dst, in_=src)
+                    for g in range(NPASS):
+                        nc.vector.quantize_mx(
+                            out=wcodes[s][:, g, half * 512:(half + 1) * 512].bitcast(FP8X4),
+                            scales=wscl[s][:, g, half * 512:(half + 1) * 512],
+                            in_=gww[:, g, :, :].rearrange("p c j -> p (c j)"),
+                        )
+                if half == 0:
+                    for i0 in range(0, 2 * NBLK, 4):
+                        cnt = min(4, 2 * NBLK - i0)
+                        bank = tp.tile([P, 4, P], F32, name="tpbank", tag="tpbank")
+                        for k in range(cnt):
+                            i = i0 + k
+                            nc.tensor.transpose(bank[:, k, :], cs[i % 2][:, i // 2, :, :].rearrange("p e j -> p (e j)"),
+                                                ident[:])
+                        nc.scalar.copy(out=csT[:, i0:i0 + cnt, :], in_=bank[:, 0:cnt, :])
+
+            for q in range(-6 - 2 * XD, -2):
+                if q % 2 == 0:
+                    prep_steps(q)
+                elif 0 <= (q + 5) // 2:
+                    turn((q + 5) // 2)
+
+        epi = ctx.enter_context(tc.tile_pool(name="epi", bufs=3))
+
+        def squares(q):
+            junk = epi.tile([P, 2 * HGRP, DH], BF16, name="junk", tag="junk", bufs=2)
+            ss = epi.tile([P, 2 * HGRP], F32, name="ss", tag="ss")
+            for s in range(2):
+                for hh in range(HGRP):
+                    i = s * HGRP + hh
+                    nc.scalar.activation(out=junk[:, i, :], in_=banks[q][s][:, DH * hh:DH * (hh + 1)],
+                                         func=ACT.Square, accum_out=ss[:, i:i + 1])
+            fl = epi.tile([P, 2 * HGRP], F32, name="fl", tag="fl")
+            nc.scalar.activation(out=fl[:], in_=ss[:], func=ACT.Relu, bias=negtiny[:, 0:1])
+            r = epi.tile([P, 2 * HGRP], F32, name="r", tag="r")
+            nc.scalar.activation(out=r[:], in_=fl[:], func=ACT.Abs_reciprocal_sqrt, bias=tiny[:, 0:1])
+            rs[q] = r
+
+        def product(q, prod, s, hh):
+            t, hg = q // 2, q % 2
+            blk = tiles[t][0]
+            nc.vector.scalar_tensor_tensor(
+                out=prod[:, hh, :, :],
+                in0=banks[q][s][:, DH * hh:DH * (hh + 1)].unsqueeze(1).to_broadcast([P, 2, DH]),
+                scalar=rs[q][:, s * HGRP + hh:s * HGRP + hh + 1],
+                in1=T[(blk, s)][:, hg * HGRP + hh, :, :],
+                op0=ALU.mult,
+                op1=ALU.mult,
+            )
+
+        with tc.manual_schedule(engines={mybir.EngineType.DVE}):
+            for q in range(-2, NQ):
+                if q + 2 < NQ:
+                    matmuls(q + 2)
+                if 0 <= q + 1 < NQ:
+                    squares(q + 1)
+                if q % 2 != 0 and (q + 5) // 2 < NT:
+                    turn((q + 5) // 2)
+                if q >= 0 and q // 8 + 1 < NBLK:
+                    table_piece(q // 8 + 1, q % 8)
+                prods = []
+                if q >= 0:
+                    for s in range(2):
+                        prod = epi.tile([P, HGRP, 2, DH], F32, name="prod%d" % s, tag="prod%d" % s)
+                        prods.append(prod)
+                    for i in range(2 * HGRP - 1):
+                        product(q, prods[i % 2], i % 2, i // 2)
+                if q % 2 == 0:
+                    prep_steps(q)
+                if q >= 0:
+                    product(q, prods[1], 1, HGRP - 1)
+                    t, hg = q // 2, q % 2
+                    blk, b = tiles[t]
+                    o = epi.tile([P, HGRP, 2, DH], F32, name="o", tag="o")
+                    step = 2 if q == NQ - 1 else HGRP
+                    for h0 in range(0, HGRP, step):
+                        nc.gpsimd.tensor_tensor(out=o[:, h0:h0 + step, :, :], in0=prods[0][:, h0:h0 + step, :, :],
+                                                in1=prods[1][:, h0:h0 + step, :, :], op=ALU.add)
+                        nc.sync.dma_start(
+                            out=out[b, hg * HGRP + h0:hg * HGRP + h0 + step, blk * P:(blk + 1) * P, :].rearrange("h n d -> n h d"),
+                            in_=o[:, h0:h0 + step, :, :].rearrange("p h e j -> p h (e j)"),
+                        )

@@ -291,16 +291,25 @@ def tile_cmattention_pa_kernel(tc, x_bytes, x_scale, a, Wq_x, Wq_a, qx_scale, qa
         def product(q, prod, s, hh):
             t, hg = q // 2, q % 2
             blk = tiles[t][0]
+            h = hg * HGRP + hh
             nc.vector.scalar_tensor_tensor(
-                out=prod[:, hh, :, :],
+                out=prod[:, h, :, :],
                 in0=banks[q][s][:, DH * hh:DH * (hh + 1)].unsqueeze(1).to_broadcast([P, 2, DH]),
                 scalar=rs[q][:, s * HGRP + hh:s * HGRP + hh + 1],
-                in1=T[(blk, s)][:, hg * HGRP + hh, :, :],
+                in1=T[(blk, s)][:, h, :, :],
                 op0=ALU.mult,
                 op1=ALU.mult,
             )
 
+        def store(t, o, h0, h1):
+            blk, b = tiles[t]
+            nc.sync.dma_start(
+                out=out[b, h0:h1, blk * P:(blk + 1) * P, :].rearrange("h n d -> n h d"),
+                in_=o[:, h0:h1, :, :].rearrange("p h e j -> p h (e j)"),
+            )
+
         with tc.manual_schedule(engines={mybir.EngineType.DVE}):
+            prods = []
             for q in range(-2, NQ):
                 if q + 2 < NQ:
                     matmuls(q + 2)
@@ -310,25 +319,28 @@ def tile_cmattention_pa_kernel(tc, x_bytes, x_scale, a, Wq_x, Wq_a, qx_scale, qa
                     turn((q + 5) // 2)
                 if q >= 0 and q // 8 + 1 < NBLK:
                     table_piece(q // 8 + 1, q % 8)
-                prods = []
                 if q >= 0:
-                    for s in range(2):
-                        prod = epi.tile([P, HGRP, 2, DH], F32, name="prod%d" % s, tag="prod%d" % s)
-                        prods.append(prod)
+                    if q % 2 == 0:
+                        prods = []
+                        for s in range(2):
+                            prod = epi.tile([P, H, 2, DH], F32, name="prod%d" % s, tag="prod%d" % s, bufs=2)
+                            prods.append(prod)
                     for i in range(2 * HGRP - 1):
                         product(q, prods[i % 2], i % 2, i // 2)
-                if q % 2 == 0:
+                if q == -2:
                     prep_steps(q)
+                elif q >= 1 and q % 2 == 1:
+                    prep_steps(q - 1)
                 if q >= 0:
                     product(q, prods[1], 1, HGRP - 1)
-                    t, hg = q // 2, q % 2
-                    blk, b = tiles[t]
-                    o = epi.tile([P, HGRP, 2, DH], F32, name="o", tag="o")
-                    step = 2 if q == NQ - 1 else HGRP
-                    for h0 in range(0, HGRP, step):
-                        nc.gpsimd.tensor_tensor(out=o[:, h0:h0 + step, :, :], in0=prods[0][:, h0:h0 + step, :, :],
-                                                in1=prods[1][:, h0:h0 + step, :, :], op=ALU.add)
-                        nc.sync.dma_start(
-                            out=out[b, hg * HGRP + h0:hg * HGRP + h0 + step, blk * P:(blk + 1) * P, :].rearrange("h n d -> n h d"),
-                            in_=o[:, h0:h0 + step, :, :].rearrange("p h e j -> p h (e j)"),
-                        )
+                    if q % 2 == 1:
+                        t = q // 2
+                        o = epi.tile([P, H, 2, DH], F32, name="o", tag="o", bufs=2)
+                        if t < NT - 1:
+                            nc.gpsimd.tensor_tensor(out=o[:], in0=prods[0][:], in1=prods[1][:], op=ALU.add)
+                            store(t, o, 0, H)
+                        else:
+                            for h0 in range(0, H, 4):
+                                nc.vector.tensor_tensor(out=o[:, h0:h0 + 4, :, :], in0=prods[0][:, h0:h0 + 4, :, :],
+                                                        in1=prods[1][:, h0:h0 + 4, :, :], op=ALU.add)
+                                store(t, o, h0, h0 + 4)

@@ -49,13 +49,20 @@ def tile_cmattention_pa_kernel(tc, x_bytes, x_scale, a, Wq_x, Wq_a, qx_scale, qa
         rs = {}
         T = {}
 
-        def load_blk(blk):
+        def load_x(blk):
             xt = ldpool.tile([P, B, D], U8, name="x8", tag="x8")
             nc.sync.dma_start(out=xt[:], in_=x_bytes[:, blk * P:(blk + 1) * P, :].rearrange("b p k -> p b k"))
             x8s[blk] = xt
-            at = ldpool.tile([P, B, D], BF16, name="a_sb", tag="a_sb")
-            nc.sync.dma_start(out=at[:], in_=a[:, blk * P:(blk + 1) * P, :].rearrange("b p k -> p b k"))
-            a_sbs[blk] = at
+
+        def load_a(blk, b0, b1):
+            if b0 == 0:
+                at = ldpool.tile([P, B, D], BF16, name="a_sb", tag="a_sb")
+                a_sbs[blk] = at
+            nc.sync.dma_start(out=a_sbs[blk][:, b0:b1, :], in_=a[b0:b1, blk * P:(blk + 1) * P, :].rearrange("b p k -> p b k"))
+
+        def load_blk(blk):
+            load_x(blk)
+            load_a(blk, 0, B)
 
         ident = const.tile([P, P], F32, name="ident")
         make_identity(nc, ident[:])
@@ -146,6 +153,10 @@ def tile_cmattention_pa_kernel(tc, x_bytes, x_scale, a, Wq_x, Wq_a, qx_scale, qa
                 for e in range(2):
                     nc.sync.dma_start(out=graw[s * H:(s + 1) * H, e * DH:(e + 1) * DH],
                                       in_=(qx_scale, qa_scale)[s].rearrange("h o j -> h (o j)"))
+            sraw = head.tile([P, P], F32, name="sraw")
+            nc.vector.memset(sraw[:], 0.0)
+            nc.sync.dma_start(out=sraw[0:D // P, :], in_=x_scale.rearrange("o q (c p) -> (o q c) p", p=P))
+            load_x(0)
             wraw = {}
 
             def load_w(s, half):
@@ -159,23 +170,28 @@ def tile_cmattention_pa_kernel(tc, x_bytes, x_scale, a, Wq_x, Wq_a, qx_scale, qa
 
             load_w(0, 0)
             load_w(1, 0)
-            gbc = []
-            for s in range(2):
-                gb = head.tile([P, H, DH], BF16, name="gbc%d" % s)
-                nc.sync.dma_start(out=gb[:].rearrange("p h j -> p (h j)"),
-                                  in_=(qx_scale, qa_scale)[s].rearrange("h o j -> (h o j)").partition_broadcast(P))
-                gbc.append(gb)
-            nc.sync.dma_start(out=xs_bc[:], in_=x_scale.rearrange("o q k -> (o q k)").partition_broadcast(P))
-            load_blk(0)
+            load_a(0, 0, 2)
             load_w(0, 1)
             load_w(1, 1)
+            load_a(0, 2, B)
             load_blk(1)
 
             gf = head.tile([P, P], F32, name="gf")
             nc.vector.tensor_copy(out=gf[:], in_=graw[:])
             gbank = tp.tile([P, 512], F32, name="tpbank", tag="tpbank")
             nc.tensor.transpose(gbank[:, 0:P], gf[:], ident[:])
+            nc.tensor.transpose(gbank[:, P:2 * P], sraw[:], ident[:])
+            scol = head.tile([P, D // P], F32, name="scol")
+            nc.scalar.copy(out=scol[:], in_=gbank[:, P:P + D // P])
             nc.scalar.copy(out=gcol[:], in_=gbank[:, 0:2 * H])
+            for c2 in range(2):
+                bank = tp.tile([P, 4, P], F32, name="tpbank", tag="tpbank")
+                for k in range(4):
+                    nc.tensor.transpose(bank[:, k, :], scol[:, 4 * c2 + k:4 * c2 + k + 1].to_broadcast([P, P]), ident[:])
+                if c2 == 0:
+                    nc.scalar.copy(out=xs_bc[:, 0:512], in_=bank[:].rearrange("p k n -> p (k n)"))
+                else:
+                    nc.vector.tensor_copy(out=xs_bc[:, 512:1024], in_=bank[:].rearrange("p k n -> p (k n)"))
 
             freq = head.tile([P, DH], F32, name="freq")
             nc.vector.memset(freq[:], 1.0)
@@ -224,12 +240,17 @@ def tile_cmattention_pa_kernel(tc, x_bytes, x_scale, a, Wq_x, Wq_a, qx_scale, qa
 
             for tab in range(2):
                 T[(0, tab)] = tabs.tile([P, H, 2, DH], F32, name="T%d" % tab, tag="T%d" % tab)
-            for h0 in (0, HGRP):
+            for h0 in range(0, H, 4):
                 for tab in range(2):
+                    bank = mm.tile([P, 4, 2, DH], F32, name="mmbank", tag="mmbank")
+                    for k in range(4):
+                        i = tab * H + h0 + k
+                        nc.tensor.transpose(bank[:, k, :, :].rearrange("p e j -> p (e j)"),
+                                            gcol[:, i:i + 1].to_broadcast([P, P]), ident[:])
                     nc.vector.tensor_tensor(
-                        out=T[(0, tab)][:, h0:h0 + HGRP, :, :],
-                        in0=gbc[tab][:, h0:h0 + HGRP, :].unsqueeze(2).to_broadcast([P, HGRP, 2, DH]),
-                        in1=cs[tab][:, 0, :, :].unsqueeze(1).to_broadcast([P, HGRP, 2, DH]),
+                        out=T[(0, tab)][:, h0:h0 + 4, :, :],
+                        in0=bank[:],
+                        in1=cs[tab][:, 0, :, :].unsqueeze(1).to_broadcast([P, 4, 2, DH]),
                         op=ALU.mult,
                     )
 

@@ -20,7 +20,7 @@ NPASS = D // 512
 HGRP = 8
 NT = B * NBLK
 NQ = 2 * NT
-XD = 3
+XD = 8
 FLOPS = 2 * 2 * B * N * D * H * DH
 
 TWO_PI = 6.283185307179586
@@ -50,7 +50,7 @@ def tile_cmattention_pa_kernel(tc, x_bytes, x_scale, a, Wq_x, Wq_a, qx_scale, qa
         T = {}
 
         def load_x(blk):
-            xt = ldpool.tile([P, B, D], U8, name="x8", tag="x8")
+            xt = ldpool.tile([P, B, D], U8, name="x8", tag="x8", bufs=NBLK)
             nc.sync.dma_start(out=xt[:], in_=x_bytes[:, blk * P:(blk + 1) * P, :].rearrange("b p k -> p b k"))
             x8s[blk] = xt
 
@@ -93,6 +93,11 @@ def tile_cmattention_pa_kernel(tc, x_bytes, x_scale, a, Wq_x, Wq_a, qx_scale, qa
                              rhs=Bm[tab][:, h0:h0 + 4, :].rearrange("p h c -> p (h c)"), start=True, stop=True)
             nc.scalar.copy(out=T[(blk, tab)][:, h0:h0 + 4, :, :].rearrange("p h e j -> p (h e j)"), in_=bank[:])
 
+        xbanks = {}
+
+        def vcopy(t):
+            return t + XD >= NT
+
         def widen(t):
             blk, b = tiles[t]
             xbf = prep.tile([P, D], BF16, name="xbf", tag="xbf", bufs=XD + 2)
@@ -106,10 +111,13 @@ def tile_cmattention_pa_kernel(tc, x_bytes, x_scale, a, Wq_x, Wq_a, qx_scale, qa
             for s in range(2):
                 bank = tp.tile([P, NPASS, 2, P], F32, name="tpbank", tag="tpbank")
                 transpose_rows(bank, srcs[s])
-                nc.scalar.copy(out=grouped[:, s, :, :, :].bitcast(F32), in_=bank[:].rearrange("p g u r -> p g r u"))
+                if s == 0 and vcopy(t):
+                    xbanks[t] = bank
+                else:
+                    nc.scalar.copy(out=grouped[:, s, :, :, :].bitcast(F32), in_=bank[:].rearrange("p g u r -> p g r u"))
             groupeds[t] = grouped
             if t % B == B - 1 and t // B + 2 < NBLK:
-                load_blk(t // B + 2)
+                load_a(t // B + 2, 0, B)
 
         def quantise(t):
             cd = prep.tile([P, 2, NPASS, P], U32, name="codes", tag="codes", bufs=3, align_bytes=64)
@@ -145,6 +153,10 @@ def tile_cmattention_pa_kernel(tc, x_bytes, x_scale, a, Wq_x, Wq_a, qx_scale, qa
                 quantise(q // 2 + 2)
             if 0 <= q // 2 + 3 + XD < NT:
                 widen(q // 2 + 3 + XD)
+            elif q // 2 + 3 in xbanks:
+                t = q // 2 + 3
+                nc.vector.tensor_copy(out=groupeds[t][:, 0, :, :, :].bitcast(F32),
+                                      in_=xbanks[t][:].rearrange("p g u r -> p g r u"))
 
         with tc.tile_pool(name="head", bufs=1) as head:
             graw = head.tile([P, P], BF16, name="graw")
@@ -174,7 +186,11 @@ def tile_cmattention_pa_kernel(tc, x_bytes, x_scale, a, Wq_x, Wq_a, qx_scale, qa
             load_w(0, 1)
             load_w(1, 1)
             load_a(0, 2, B)
-            load_blk(1)
+            load_x(1)
+            load_x(2)
+            load_a(1, 0, B)
+            load_x(3)
+            load_x(4)
 
             gf = head.tile([P, P], F32, name="gf")
             nc.vector.tensor_copy(out=gf[:], in_=graw[:])
@@ -287,11 +303,13 @@ def tile_cmattention_pa_kernel(tc, x_bytes, x_scale, a, Wq_x, Wq_a, qx_scale, qa
                                                 ident[:])
                         nc.scalar.copy(out=csT[:, i0:i0 + cnt, :], in_=bank[:, 0:cnt, :])
 
-            for q in range(-6 - 2 * XD, -2):
-                if q % 2 == 0:
-                    prep_steps(q)
-                elif 0 <= (q + 5) // 2:
-                    turn((q + 5) // 2)
+            for t in range(3):
+                widen(t)
+            turn(0)
+            quantise(0)
+            turn(1)
+            for t in range(3, XD + 2):
+                widen(t)
 
         epi = ctx.enter_context(tc.tile_pool(name="epi", bufs=3))
 
@@ -336,10 +354,10 @@ def tile_cmattention_pa_kernel(tc, x_bytes, x_scale, a, Wq_x, Wq_a, qx_scale, qa
                     matmuls(q + 2)
                 if 0 <= q + 1 < NQ:
                     squares(q + 1)
-                if q % 2 != 0 and (q + 5) // 2 < NT:
-                    turn((q + 5) // 2)
                 if q >= 0 and q // 8 + 1 < NBLK:
                     table_piece(q // 8 + 1, q % 8)
+                if q % 2 != 0 and (q + 5) // 2 < NT:
+                    turn((q + 5) // 2)
                 if q >= 0:
                     if q % 2 == 0:
                         prods = []

@@ -20,7 +20,7 @@ NPASS = D // 512
 HGRP = 8
 NT = B * NBLK
 NQ = 2 * NT
-XD = 8
+XD = 12
 FLOPS = 2 * 2 * B * N * D * H * DH
 
 TWO_PI = 6.283185307179586
@@ -71,10 +71,12 @@ def tile_cmattention_pa_kernel(tc, x_bytes, x_scale, a, Wq_x, Wq_a, qx_scale, qa
         negtiny = const.tile([P, 1], F32, name="negtiny")
         nc.vector.memset(negtiny[:], -1e-24)
         xs_bc = const.tile([P, D], F32, name="xs_bc")
-        cs = [const.tile([P, NBLK, 2, DH], F32, name="cs%d" % tab) for tab in range(2)]
-        csT = const.tile([P, 2 * NBLK, P], F32, name="csT")
+        identb = const.tile([P, P], BF16, name="identb")
+        make_identity(nc, identb[:])
+        NFN = 3
+        csT = const.tile([P, NFN * NBLK, P], BF16, name="csT")
         gcol = const.tile([P, 2 * H], F32, name="gcol")
-        Bm = [const.tile([P, H, P], F32, name="Bm%d" % tab) for tab in range(2)]
+        Bg = [const.tile([P, H, DH], BF16, name="Bg%d" % v) for v in range(2)]
         wcodes = [const.tile([P, NPASS, H * DH], U32, name="wcodes%d" % s, align_bytes=64) for s in range(2)]
         wscl = [const.tile([P, NPASS, H * DH], U8, name="wscl%d" % s, align_bytes=64) for s in range(2)]
 
@@ -84,14 +86,16 @@ def tile_cmattention_pa_kernel(tc, x_bytes, x_scale, a, Wq_x, Wq_a, qx_scale, qa
                     nc.tensor.transpose(bank[:, g, u, :], words[:, 256 * g + u:256 * (g + 1):2], ident[:])
 
         def table_piece(blk, i):
-            tab = i // 4
-            h0 = 4 * (i % 4)
+            h0 = HGRP * (i // 4)
+            tab = (i // 2) % 2
+            e = i % 2
+            fn = e if tab == 0 else 2 - 2 * e
             if (blk, tab) not in T:
                 T[(blk, tab)] = tabs.tile([P, H, 2, DH], F32, name="T%d" % tab, tag="T%d" % tab)
             bank = tp.tile([P, 512], F32, name="tpbank", tag="tpbank")
-            nc.tensor.matmul(out=bank[:], lhsT=csT[:, 2 * blk + tab, :],
-                             rhs=Bm[tab][:, h0:h0 + 4, :].rearrange("p h c -> p (h c)"), start=True, stop=True)
-            nc.scalar.copy(out=T[(blk, tab)][:, h0:h0 + 4, :, :].rearrange("p h e j -> p (h e j)"), in_=bank[:])
+            nc.tensor.matmul(out=bank[:], lhsT=csT[:, NFN * blk + fn, :],
+                             rhs=Bg[tab][:, h0:h0 + HGRP, :].rearrange("p h j -> p (h j)"), start=True, stop=True)
+            nc.scalar.copy(out=T[(blk, tab)][:, h0:h0 + HGRP, e, :], in_=bank[:].rearrange("p (h j) -> p h j", j=DH))
 
         xbanks = {}
 
@@ -153,10 +157,7 @@ def tile_cmattention_pa_kernel(tc, x_bytes, x_scale, a, Wq_x, Wq_a, qx_scale, qa
                 quantise(q // 2 + 2)
             if 0 <= q // 2 + 3 + XD < NT:
                 widen(q // 2 + 3 + XD)
-            elif q // 2 + 3 in xbanks:
-                t = q // 2 + 3
-                nc.vector.tensor_copy(out=groupeds[t][:, 0, :, :, :].bitcast(F32),
-                                      in_=xbanks[t][:].rearrange("p g u r -> p g r u"))
+
 
         with tc.tile_pool(name="head", bufs=1) as head:
             graw = head.tile([P, P], BF16, name="graw")
@@ -204,10 +205,14 @@ def tile_cmattention_pa_kernel(tc, x_bytes, x_scale, a, Wq_x, Wq_a, qx_scale, qa
                 bank = tp.tile([P, 4, P], F32, name="tpbank", tag="tpbank")
                 for k in range(4):
                     nc.tensor.transpose(bank[:, k, :], scol[:, 4 * c2 + k:4 * c2 + k + 1].to_broadcast([P, P]), ident[:])
-                if c2 == 0:
-                    nc.scalar.copy(out=xs_bc[:, 0:512], in_=bank[:].rearrange("p k n -> p (k n)"))
-                else:
-                    nc.vector.tensor_copy(out=xs_bc[:, 512:1024], in_=bank[:].rearrange("p k n -> p (k n)"))
+                nc.scalar.copy(out=xs_bc[:, c2 * 512:(c2 + 1) * 512], in_=bank[:].rearrange("p k n -> p (k n)"))
+
+            id2 = head.tile([P, DH], BF16, name="id2")
+            nc.vector.tensor_tensor(out=id2[:], in0=ident[:, 0:DH], in1=ident[:, DH:P], op=ALU.add)
+            for h in range(H):
+                for v in range(2):
+                    nc.scalar.activation(out=Bg[v][:, h, :], in_=id2[:], func=ACT.Copy,
+                                         scale=gcol[:, v * H + h:v * H + h + 1])
 
             freq = head.tile([P, DH], F32, name="freq")
             nc.vector.memset(freq[:], 1.0)
@@ -239,41 +244,23 @@ def tile_cmattention_pa_kernel(tc, x_bytes, x_scale, a, Wq_x, Wq_a, qx_scale, qa
             nc.scalar.activation(out=s2[:], in_=red[:], func=ACT.Sin, scale=0.5)
             s4 = head.tile([P, NBLK, DH], F32, name="s4")
             nc.scalar.activation(out=s4[:], in_=red[:], func=ACT.Sin, scale=0.25)
+            warm = head.tile([P, 1], F32, name="warm")
+            nc.scalar.activation(out=warm[:], in_=tiny[:], func=ACT.Abs_reciprocal_sqrt)
             q2 = head.tile([P, NBLK, DH], F32, name="q2")
             nc.vector.tensor_tensor(out=q2[:], in0=s2[:], in1=s2[:], op=ALU.mult)
-            nc.vector.tensor_scalar(out=cs[0][:, :, 0, :], in0=q2[:], scalar1=-2.0, scalar2=1.0,
-                                    op0=ALU.mult, op1=ALU.add)
-            nc.vector.tensor_scalar(out=cs[1][:, :, 1, :], in0=q2[:], scalar1=-2.0, scalar2=1.0,
+            trig = head.tile([P, NBLK, 2, DH], F32, name="trig")
+            nc.vector.tensor_scalar(out=trig[:, :, 0, :], in0=q2[:], scalar1=-2.0, scalar2=1.0,
                                     op0=ALU.mult, op1=ALU.add)
             q4 = head.tile([P, NBLK, DH], F32, name="q4")
             nc.vector.tensor_tensor(out=q4[:], in0=s4[:], in1=s4[:], op=ALU.mult)
             c2 = head.tile([P, NBLK, DH], F32, name="c2")
             nc.vector.tensor_scalar(out=c2[:], in0=q4[:], scalar1=-2.0, scalar2=1.0, op0=ALU.mult, op1=ALU.add)
-            nc.vector.scalar_tensor_tensor(out=cs[0][:, :, 1, :], in0=s2[:], scalar=2.0, in1=c2[:],
+            nc.vector.scalar_tensor_tensor(out=trig[:, :, 1, :], in0=s2[:], scalar=2.0, in1=c2[:],
                                            op0=ALU.mult, op1=ALU.mult)
-            nc.vector.scalar_tensor_tensor(out=cs[1][:, :, 0, :], in0=s2[:], scalar=-2.0, in1=c2[:],
-                                           op0=ALU.mult, op1=ALU.mult)
-
-            for tab in range(2):
-                T[(0, tab)] = tabs.tile([P, H, 2, DH], F32, name="T%d" % tab, tag="T%d" % tab)
-            for h0 in range(0, H, 4):
-                for tab in range(2):
-                    bank = mm.tile([P, 4, 2, DH], F32, name="mmbank", tag="mmbank")
-                    for k in range(4):
-                        i = tab * H + h0 + k
-                        nc.tensor.transpose(bank[:, k, :, :].rearrange("p e j -> p (e j)"),
-                                            gcol[:, i:i + 1].to_broadcast([P, P]), ident[:])
-                    nc.vector.tensor_tensor(
-                        out=T[(0, tab)][:, h0:h0 + 4, :, :],
-                        in0=bank[:],
-                        in1=cs[tab][:, 0, :, :].unsqueeze(1).to_broadcast([P, 4, 2, DH]),
-                        op=ALU.mult,
-                    )
-
-            for h in range(H):
-                for tab in range(2):
-                    nc.scalar.activation(out=Bm[tab][:, h, :], in_=ident[:], func=ACT.Copy,
-                                         scale=gcol[:, tab * H + h:tab * H + h + 1])
+            hl = head.tile([P, NBLK, NFN, 2, DH], BF16, name="hl")
+            nc.vector.tensor_copy(out=hl[:, :, 0:2, 0, :], in_=trig[:])
+            nc.vector.tensor_tensor(out=hl[:, :, 0:2, 1, :], in0=trig[:], in1=hl[:, :, 0:2, 0, :], op=ALU.subtract)
+            nc.vector.tensor_scalar_mul(out=hl[:, :, 2, :, :], in0=hl[:, :, 1, :, :], scalar1=-1.0)
 
             for half in range(2):
                 for s in range(2):
@@ -283,7 +270,7 @@ def tile_cmattention_pa_kernel(tc, x_bytes, x_scale, a, Wq_x, Wq_a, qx_scale, qa
                         transpose_rows(bank, wraw[(s, half)][:, rr, :].bitcast(F32))
                         dst = gww[:, :, rr * P:(rr + 1) * P, :].bitcast(F32)
                         src = bank[:].rearrange("p g u r -> p g r u")
-                        if rr % 2 == 0:
+                        if rr < 0:
                             nc.vector.tensor_copy(out=dst, in_=src)
                         else:
                             nc.scalar.copy(out=dst, in_=src)
@@ -294,14 +281,19 @@ def tile_cmattention_pa_kernel(tc, x_bytes, x_scale, a, Wq_x, Wq_a, qx_scale, qa
                             in_=gww[:, g, :, :].rearrange("p c j -> p (c j)"),
                         )
                 if half == 0:
-                    for i0 in range(0, 2 * NBLK, 4):
-                        cnt = min(4, 2 * NBLK - i0)
-                        bank = tp.tile([P, 4, P], F32, name="tpbank", tag="tpbank")
+                    for i0 in range(0, NFN * NBLK, 4):
+                        cnt = min(4, NFN * NBLK - i0)
+                        bank = tp.tile([P, 4, P], BF16, name="tpbank", tag="tpbank")
                         for k in range(cnt):
                             i = i0 + k
-                            nc.tensor.transpose(bank[:, k, :], cs[i % 2][:, i // 2, :, :].rearrange("p e j -> p (e j)"),
-                                                ident[:])
+                            nc.tensor.transpose(bank[:, k, :], hl[:, i // NFN, i % NFN, :, :].rearrange("p t j -> p (t j)"),
+                                                identb[:])
                         nc.scalar.copy(out=csT[:, i0:i0 + cnt, :], in_=bank[:, 0:cnt, :])
+                    for i in range(4):
+                        table_piece(0, i)
+                else:
+                    for i in range(4, 8):
+                        table_piece(0, i)
 
             for t in range(3):
                 widen(t)
@@ -366,6 +358,10 @@ def tile_cmattention_pa_kernel(tc, x_bytes, x_scale, a, Wq_x, Wq_a, qx_scale, qa
                             prods.append(prod)
                     for i in range(2 * HGRP - 1):
                         product(q, prods[i % 2], i % 2, i // 2)
+                        if i == 11 and (q + 5) // 2 in xbanks and q % 2 == 1:
+                            tx = (q + 5) // 2
+                            nc.vector.tensor_copy(out=groupeds[tx][:, 0, :, :, :].bitcast(F32),
+                                                  in_=xbanks[tx][:].rearrange("p g u r -> p g r u"))
                 if q == -2:
                     prep_steps(q)
                 elif q >= 1 and q % 2 == 1:

@@ -20,7 +20,7 @@ NPASS = D // 512
 HGRP = 8
 NT = B * NBLK
 NQ = 2 * NT
-XD = 12
+XD = 16
 FLOPS = 2 * 2 * B * N * D * H * DH
 
 TWO_PI = 6.283185307179586

@@ -20,7 +20,7 @@ NPASS = D // 512
 HGRP = 8
 NT = B * NBLK
 NQ = 2 * NT
-XD = 16
+XD = 9
 FLOPS = 2 * 2 * B * N * D * H * DH
 
 TWO_PI = 6.283185307179586
@@ -47,6 +47,8 @@ def tile_cmattention_pa_kernel(tc, x_bytes, x_scale, a, Wq_x, Wq_a, qx_scale, qa
         codes = {}
         banks = {}
         rs = {}
+        sums = {}
+        clamped = {}
         T = {}
 
         def load_x(blk):
@@ -68,6 +70,8 @@ def tile_cmattention_pa_kernel(tc, x_bytes, x_scale, a, Wq_x, Wq_a, qx_scale, qa
         make_identity(nc, ident[:])
         tiny = const.tile([P, 1], F32, name="tiny")
         nc.vector.memset(tiny[:], 1e-24)
+        warm0 = const.tile([P, 1], F32, name="warm0")
+        nc.scalar.activation(out=warm0[:], in_=tiny[:], func=ACT.Sin)
         negtiny = const.tile([P, 1], F32, name="negtiny")
         nc.vector.memset(negtiny[:], -1e-24)
         xs_bc = const.tile([P, D], F32, name="xs_bc")
@@ -85,7 +89,7 @@ def tile_cmattention_pa_kernel(tc, x_bytes, x_scale, a, Wq_x, Wq_a, qx_scale, qa
                 for u in range(2):
                     nc.tensor.transpose(bank[:, g, u, :], words[:, 256 * g + u:256 * (g + 1):2], ident[:])
 
-        def table_piece(blk, i):
+        def table_piece(blk, i, on_vector=False):
             h0 = HGRP * (i // 4)
             tab = (i // 2) % 2
             e = i % 2
@@ -95,12 +99,17 @@ def tile_cmattention_pa_kernel(tc, x_bytes, x_scale, a, Wq_x, Wq_a, qx_scale, qa
             bank = tp.tile([P, 512], F32, name="tpbank", tag="tpbank")
             nc.tensor.matmul(out=bank[:], lhsT=csT[:, NFN * blk + fn, :],
                              rhs=Bg[tab][:, h0:h0 + HGRP, :].rearrange("p h j -> p (h j)"), start=True, stop=True)
-            nc.scalar.copy(out=T[(blk, tab)][:, h0:h0 + HGRP, e, :], in_=bank[:].rearrange("p (h j) -> p h j", j=DH))
+            dst = T[(blk, tab)][:, h0:h0 + HGRP, e, :]
+            src = bank[:].rearrange("p (h j) -> p h j", j=DH)
+            if on_vector:
+                nc.vector.tensor_copy(out=dst, in_=src)
+            else:
+                nc.scalar.copy(out=dst, in_=src)
 
         xbanks = {}
 
         def vcopy(t):
-            return t + XD >= NT
+            return False
 
         def widen(t):
             blk, b = tiles[t]
@@ -108,19 +117,19 @@ def tile_cmattention_pa_kernel(tc, x_bytes, x_scale, a, Wq_x, Wq_a, qx_scale, qa
             nc.vector.tensor_tensor(out=xbf[:], in0=x8s[blk][:, b, :].bitcast(FP8), in1=xs_bc[:], op=ALU.mult)
             xbfs[t] = xbf
 
-        def turn(t):
+        def turn_half(t, s):
             blk, b = tiles[t]
-            grouped = prep.tile([P, 2, NPASS, P, 4], BF16, name="grouped", tag="grouped", align_bytes=64)
-            srcs = (xbfs[t][:].bitcast(F32), a_sbs[blk][:, b, :].bitcast(F32))
-            for s in range(2):
-                bank = tp.tile([P, NPASS, 2, P], F32, name="tpbank", tag="tpbank")
-                transpose_rows(bank, srcs[s])
-                if s == 0 and vcopy(t):
-                    xbanks[t] = bank
-                else:
-                    nc.scalar.copy(out=grouped[:, s, :, :, :].bitcast(F32), in_=bank[:].rearrange("p g u r -> p g r u"))
-            groupeds[t] = grouped
-            if t % B == B - 1 and t // B + 2 < NBLK:
+            if s == 0:
+                grouped = prep.tile([P, 2, NPASS, P, 4], BF16, name="grouped", tag="grouped", align_bytes=64)
+                groupeds[t] = grouped
+            src = xbfs[t][:].bitcast(F32) if s == 0 else a_sbs[blk][:, b, :].bitcast(F32)
+            bank = tp.tile([P, NPASS, 2, P], F32, name="tpbank", tag="tpbank")
+            transpose_rows(bank, src)
+            if s == 0 and vcopy(t):
+                xbanks[t] = bank
+            else:
+                nc.scalar.copy(out=groupeds[t][:, s, :, :, :].bitcast(F32), in_=bank[:].rearrange("p g u r -> p g r u"))
+            if s == 1 and t % B == B - 1 and t // B + 2 < NBLK:
                 load_a(t // B + 2, 0, B)
 
         def quantise(t):
@@ -158,6 +167,8 @@ def tile_cmattention_pa_kernel(tc, x_bytes, x_scale, a, Wq_x, Wq_a, qx_scale, qa
             if 0 <= q // 2 + 3 + XD < NT:
                 widen(q // 2 + 3 + XD)
 
+
+        sq = ctx.enter_context(tc.tile_pool(name="sq", bufs=3))
 
         with tc.tile_pool(name="head", bufs=1) as head:
             graw = head.tile([P, P], BF16, name="graw")
@@ -209,10 +220,9 @@ def tile_cmattention_pa_kernel(tc, x_bytes, x_scale, a, Wq_x, Wq_a, qx_scale, qa
 
             id2 = head.tile([P, DH], BF16, name="id2")
             nc.vector.tensor_tensor(out=id2[:], in0=ident[:, 0:DH], in1=ident[:, DH:P], op=ALU.add)
-            for h in range(H):
-                for v in range(2):
-                    nc.scalar.activation(out=Bg[v][:, h, :], in_=id2[:], func=ACT.Copy,
-                                         scale=gcol[:, v * H + h:v * H + h + 1])
+            for v in range(2):
+                nc.gpsimd.tensor_tensor(out=Bg[v][:], in0=id2[:].unsqueeze(1).to_broadcast([P, H, DH]),
+                                        in1=gcol[:, v * H:(v + 1) * H].unsqueeze(2).to_broadcast([P, H, DH]), op=ALU.mult)
 
             freq = head.tile([P, DH], F32, name="freq")
             nc.vector.memset(freq[:], 1.0)
@@ -222,41 +232,27 @@ def tile_cmattention_pa_kernel(tc, x_bytes, x_scale, a, Wq_x, Wq_a, qx_scale, qa
                 nc.vector.tensor_scalar_mul(out=view, in0=view, scalar1=10000.0 ** (-c / 64.0))
             n_i = head.tile([P, NBLK], I32, name="n_i")
             nc.gpsimd.iota(n_i[:], pattern=[[P, NBLK]], base=0, channel_multiplier=1)
-            n_f = head.tile([P, NBLK], F32, name="n_f")
-            nc.vector.tensor_copy(out=n_f[:], in_=n_i[:])
             theta = head.tile([P, NBLK, DH], F32, name="theta")
-            nc.vector.tensor_tensor(out=theta[:], in0=freq[:].unsqueeze(1).to_broadcast([P, NBLK, DH]),
-                                    in1=n_f[:].unsqueeze(2).to_broadcast([P, NBLK, DH]), op=ALU.mult)
-            turns = head.tile([P, NBLK, DH], F32, name="turns")
-            nc.vector.tensor_scalar(out=turns[:], in0=theta[:], scalar1=1.0 / TWO_PI, scalar2=0.25,
-                                    op0=ALU.mult, op1=ALU.add)
+            nc.vector.tensor_tensor(out=theta[:], in0=n_i[:].unsqueeze(2).to_broadcast([P, NBLK, DH]),
+                                    in1=freq[:].unsqueeze(1).to_broadcast([P, NBLK, DH]), op=ALU.mult)
             k_i = head.tile([P, NBLK, DH], I32, name="k_i")
-            nc.vector.tensor_copy(out=k_i[:], in_=turns[:])
-            k_f = head.tile([P, NBLK, DH], F32, name="k_f")
-            nc.vector.tensor_copy(out=k_f[:], in_=k_i[:])
+            nc.vector.tensor_scalar_mul(out=k_i[:], in0=theta[:], scalar1=1.0 / TWO_PI)
             red1 = head.tile([P, NBLK, DH], F32, name="red1")
-            nc.vector.scalar_tensor_tensor(out=red1[:], in0=k_f[:], scalar=-C1, in1=theta[:],
+            nc.vector.scalar_tensor_tensor(out=red1[:], in0=k_i[:], scalar=-C1, in1=theta[:],
                                            op0=ALU.mult, op1=ALU.add)
             red = head.tile([P, NBLK, DH], F32, name="red")
-            nc.vector.scalar_tensor_tensor(out=red[:], in0=k_f[:], scalar=-C2, in1=red1[:],
+            nc.vector.scalar_tensor_tensor(out=red[:], in0=k_i[:], scalar=-C2, in1=red1[:],
                                            op0=ALU.mult, op1=ALU.add)
+            trig = head.tile([P, NBLK, 2, DH], F32, name="trig")
             s2 = head.tile([P, NBLK, DH], F32, name="s2")
             nc.scalar.activation(out=s2[:], in_=red[:], func=ACT.Sin, scale=0.5)
-            s4 = head.tile([P, NBLK, DH], F32, name="s4")
-            nc.scalar.activation(out=s4[:], in_=red[:], func=ACT.Sin, scale=0.25)
+            nc.scalar.activation(out=trig[:, :, 1, :], in_=red[:], func=ACT.Sin)
             warm = head.tile([P, 1], F32, name="warm")
-            nc.scalar.activation(out=warm[:], in_=tiny[:], func=ACT.Abs_reciprocal_sqrt)
+            nc.scalar.activation(out=warm[:], in_=trig[:, 0, 1, 0:1], func=ACT.Abs_reciprocal_sqrt, bias=tiny[:, 0:1])
             q2 = head.tile([P, NBLK, DH], F32, name="q2")
             nc.vector.tensor_tensor(out=q2[:], in0=s2[:], in1=s2[:], op=ALU.mult)
-            trig = head.tile([P, NBLK, 2, DH], F32, name="trig")
             nc.vector.tensor_scalar(out=trig[:, :, 0, :], in0=q2[:], scalar1=-2.0, scalar2=1.0,
                                     op0=ALU.mult, op1=ALU.add)
-            q4 = head.tile([P, NBLK, DH], F32, name="q4")
-            nc.vector.tensor_tensor(out=q4[:], in0=s4[:], in1=s4[:], op=ALU.mult)
-            c2 = head.tile([P, NBLK, DH], F32, name="c2")
-            nc.vector.tensor_scalar(out=c2[:], in0=q4[:], scalar1=-2.0, scalar2=1.0, op0=ALU.mult, op1=ALU.add)
-            nc.vector.scalar_tensor_tensor(out=trig[:, :, 1, :], in0=s2[:], scalar=2.0, in1=c2[:],
-                                           op0=ALU.mult, op1=ALU.mult)
             hl = head.tile([P, NBLK, NFN, 2, DH], BF16, name="hl")
             nc.vector.tensor_copy(out=hl[:, :, 0:2, 0, :], in_=trig[:])
             nc.vector.tensor_tensor(out=hl[:, :, 0:2, 1, :], in0=trig[:], in1=hl[:, :, 0:2, 0, :], op=ALU.subtract)
@@ -291,32 +287,39 @@ def tile_cmattention_pa_kernel(tc, x_bytes, x_scale, a, Wq_x, Wq_a, qx_scale, qa
                         nc.scalar.copy(out=csT[:, i0:i0 + cnt, :], in_=bank[:, 0:cnt, :])
                     for i in range(4):
                         table_piece(0, i)
-                else:
-                    for i in range(4, 8):
-                        table_piece(0, i)
+                    for t in range(2):
+                        widen(t)
+                    turn_half(0, 0)
+                    turn_half(0, 1)
+                    quantise(0)
 
-            for t in range(3):
-                widen(t)
-            turn(0)
-            quantise(0)
-            turn(1)
-            for t in range(3, XD + 2):
+            for i in range(4, 8):
+                table_piece(0, i, on_vector=True)
+            turn_half(1, 0)
+            turn_half(1, 1)
+            for t in range(2, XD + 2):
                 widen(t)
 
         epi = ctx.enter_context(tc.tile_pool(name="epi", bufs=3))
 
         def squares(q):
-            junk = epi.tile([P, 2 * HGRP, DH], BF16, name="junk", tag="junk", bufs=2)
-            ss = epi.tile([P, 2 * HGRP], F32, name="ss", tag="ss")
+            junk = sq.tile([P, 2 * HGRP, DH], BF16, name="junk", tag="junk", bufs=2)
+            ss = sq.tile([P, 2 * HGRP], F32, name="ss", tag="ss")
             for s in range(2):
                 for hh in range(HGRP):
                     i = s * HGRP + hh
                     nc.scalar.activation(out=junk[:, i, :], in_=banks[q][s][:, DH * hh:DH * (hh + 1)],
                                          func=ACT.Square, accum_out=ss[:, i:i + 1])
-            fl = epi.tile([P, 2 * HGRP], F32, name="fl", tag="fl")
-            nc.scalar.activation(out=fl[:], in_=ss[:], func=ACT.Relu, bias=negtiny[:, 0:1])
-            r = epi.tile([P, 2 * HGRP], F32, name="r", tag="r")
-            nc.scalar.activation(out=r[:], in_=fl[:], func=ACT.Abs_reciprocal_sqrt, bias=tiny[:, 0:1])
+            sums[q] = ss
+
+        def clamp(q):
+            fl = sq.tile([P, 2 * HGRP], F32, name="fl", tag="fl")
+            nc.scalar.activation(out=fl[:], in_=sums[q][:], func=ACT.Relu, bias=negtiny[:, 0:1])
+            clamped[q] = fl
+
+        def root(q):
+            r = sq.tile([P, 2 * HGRP], F32, name="r", tag="r")
+            nc.scalar.activation(out=r[:], in_=clamped[q][:], func=ACT.Abs_reciprocal_sqrt, bias=tiny[:, 0:1])
             rs[q] = r
 
         def product(q, prod, s, hh):
@@ -339,17 +342,28 @@ def tile_cmattention_pa_kernel(tc, x_bytes, x_scale, a, Wq_x, Wq_a, qx_scale, qa
                 in_=o[:, h0:h1, :, :].rearrange("p h e j -> p h (e j)"),
             )
 
-        with tc.manual_schedule(engines={mybir.EngineType.DVE}):
+        with tc.manual_schedule(engines={mybir.EngineType.DVE, mybir.EngineType.PE, mybir.EngineType.Activation}):
             prods = []
             for q in range(-2, NQ):
-                if q + 2 < NQ:
+                if q < 0:
                     matmuls(q + 2)
                 if 0 <= q + 1 < NQ:
                     squares(q + 1)
-                if q >= 0 and q // 8 + 1 < NBLK:
-                    table_piece(q // 8 + 1, q % 8)
-                if q % 2 != 0 and (q + 5) // 2 < NT:
-                    turn((q + 5) // 2)
+                if q == -1:
+                    clamp(0)
+                    root(0)
+                    turn_half(2, 0)
+                if q >= 0:
+                    if q // 8 + 1 < NBLK:
+                        table_piece(q // 8 + 1, q % 8)
+                    if q + 1 < NQ:
+                        clamp(q + 1)
+                    if (q + 4 + q % 2) // 2 < NT:
+                        turn_half((q + 4 + q % 2) // 2, (q + 1) % 2)
+                    if q + 1 < NQ:
+                        root(q + 1)
+                    if q + 2 < NQ:
+                        matmuls(q + 2)
                 if q >= 0:
                     if q % 2 == 0:
                         prods = []

@@ -20,7 +20,7 @@ NPASS = D // 512
 HGRP = 8
 NT = B * NBLK
 NQ = 2 * NT
-XD = 9
+NHEAD = 12
 FLOPS = 2 * 2 * B * N * D * H * DH
 
 TWO_PI = 6.283185307179586
@@ -113,7 +113,7 @@ def tile_cmattention_pa_kernel(tc, x_bytes, x_scale, a, Wq_x, Wq_a, qx_scale, qa
 
         def widen(t):
             blk, b = tiles[t]
-            xbf = prep.tile([P, D], BF16, name="xbf", tag="xbf", bufs=XD + 2)
+            xbf = prep.tile([P, D], BF16, name="xbf", tag="xbf", bufs=NHEAD + 1)
             nc.vector.tensor_tensor(out=xbf[:], in0=x8s[blk][:, b, :].bitcast(FP8), in1=xs_bc[:], op=ALU.mult)
             xbfs[t] = xbf
 
@@ -164,8 +164,8 @@ def tile_cmattention_pa_kernel(tc, x_bytes, x_scale, a, Wq_x, Wq_a, qx_scale, qa
         def prep_steps(q):
             if 0 <= q // 2 + 2 < NT:
                 quantise(q // 2 + 2)
-            if 0 <= q // 2 + 3 + XD < NT:
-                widen(q // 2 + 3 + XD)
+            if q >= 0 and q // 2 % 2 == 1 and NHEAD + q // 4 < NT:
+                widen(NHEAD + q // 4)
 
 
         sq = ctx.enter_context(tc.tile_pool(name="sq", bufs=3))
@@ -297,7 +297,7 @@ def tile_cmattention_pa_kernel(tc, x_bytes, x_scale, a, Wq_x, Wq_a, qx_scale, qa
                 table_piece(0, i, on_vector=True)
             turn_half(1, 0)
             turn_half(1, 1)
-            for t in range(2, XD + 2):
+            for t in range(2, NHEAD):
                 widen(t)
 
         epi = ctx.enter_context(tc.tile_pool(name="epi", bufs=3))

@@ -111,11 +111,13 @@ def tile_cmattention_pa_kernel(tc, x_bytes, x_scale, a, Wq_x, Wq_a, qx_scale, qa
         def vcopy(t):
             return False
 
-        def widen(t):
+        def widen(t, k0=0, k1=D):
             blk, b = tiles[t]
-            xbf = prep.tile([P, D], BF16, name="xbf", tag="xbf", bufs=NHEAD + 1)
-            nc.vector.tensor_tensor(out=xbf[:], in0=x8s[blk][:, b, :].bitcast(FP8), in1=xs_bc[:], op=ALU.mult)
-            xbfs[t] = xbf
+            if k0 == 0:
+                xbf = prep.tile([P, D], BF16, name="xbf", tag="xbf", bufs=NHEAD + 1)
+                xbfs[t] = xbf
+            nc.vector.tensor_tensor(out=xbfs[t][:, k0:k1], in0=x8s[blk][:, b, k0:k1].bitcast(FP8),
+                                    in1=xs_bc[:, k0:k1], op=ALU.mult)
 
         def turn_half(t, s):
             blk, b = tiles[t]
@@ -164,8 +166,8 @@ def tile_cmattention_pa_kernel(tc, x_bytes, x_scale, a, Wq_x, Wq_a, qx_scale, qa
         def prep_steps(q):
             if 0 <= q // 2 + 2 < NT:
                 quantise(q // 2 + 2)
-            if q >= 0 and q // 2 % 2 == 1 and NHEAD + q // 4 < NT:
-                widen(NHEAD + q // 4)
+            if q >= 0 and NHEAD + q // 4 < NT:
+                widen(NHEAD + q // 4, D // 2 * (q // 2 % 2), D // 2 * (q // 2 % 2) + D // 2)
 
 
         sq = ctx.enter_context(tc.tile_pool(name="sq", bufs=3))
@@ -212,17 +214,18 @@ def tile_cmattention_pa_kernel(tc, x_bytes, x_scale, a, Wq_x, Wq_a, qx_scale, qa
             scol = head.tile([P, D // P], F32, name="scol")
             nc.scalar.copy(out=scol[:], in_=gbank[:, P:P + D // P])
             nc.scalar.copy(out=gcol[:], in_=gbank[:, 0:2 * H])
+            id2 = head.tile([P, DH], BF16, name="id2")
+            nc.vector.tensor_tensor(out=id2[:], in0=ident[:, 0:DH], in1=ident[:, DH:P], op=ALU.add)
+            nc.vector.tensor_tensor(out=Bg[0][:], in0=id2[:].unsqueeze(1).to_broadcast([P, H, DH]),
+                                    in1=gcol[:, 0:H].unsqueeze(2).to_broadcast([P, H, DH]), op=ALU.mult)
+            for h in range(H):
+                nc.scalar.activation(out=Bg[1][:, h, :], in_=id2[:], func=ACT.Copy, scale=gcol[:, H + h:H + h + 1])
+
             for c2 in range(2):
                 bank = tp.tile([P, 4, P], F32, name="tpbank", tag="tpbank")
                 for k in range(4):
                     nc.tensor.transpose(bank[:, k, :], scol[:, 4 * c2 + k:4 * c2 + k + 1].to_broadcast([P, P]), ident[:])
                 nc.scalar.copy(out=xs_bc[:, c2 * 512:(c2 + 1) * 512], in_=bank[:].rearrange("p k n -> p (k n)"))
-
-            id2 = head.tile([P, DH], BF16, name="id2")
-            nc.vector.tensor_tensor(out=id2[:], in0=ident[:, 0:DH], in1=ident[:, DH:P], op=ALU.add)
-            for v in range(2):
-                nc.gpsimd.tensor_tensor(out=Bg[v][:], in0=id2[:].unsqueeze(1).to_broadcast([P, H, DH]),
-                                        in1=gcol[:, v * H:(v + 1) * H].unsqueeze(2).to_broadcast([P, H, DH]), op=ALU.mult)
 
             freq = head.tile([P, DH], F32, name="freq")
             nc.vector.memset(freq[:], 1.0)

@@ -96,7 +96,10 @@ def tile_cmattention_pa_kernel(tc, x_bytes, x_scale, a, Wq_x, Wq_a, qx_scale, qa
             fn = e if tab == 0 else 2 - 2 * e
             if (blk, tab) not in T:
                 T[(blk, tab)] = tabs.tile([P, H, 2, DH], F32, name="T%d" % tab, tag="T%d" % tab)
-            bank = tp.tile([P, 512], F32, name="tpbank", tag="tpbank")
+            if on_vector:
+                bank = mm.tile([P, 512], F32, name="mmbank", tag="mmbank")
+            else:
+                bank = tp.tile([P, 512], F32, name="tpbank", tag="tpbank")
             nc.tensor.matmul(out=bank[:], lhsT=csT[:, NFN * blk + fn, :],
                              rhs=Bg[tab][:, h0:h0 + HGRP, :].rearrange("p h j -> p (h j)"), start=True, stop=True)
             dst = T[(blk, tab)][:, h0:h0 + HGRP, e, :]
@@ -164,9 +167,9 @@ def tile_cmattention_pa_kernel(tc, x_bytes, x_scale, a, Wq_x, Wq_a, qx_scale, qa
             banks[q] = pair
 
         def prep_steps(q):
-            if 0 <= q // 2 + 2 < NT:
+            if q // 2 + 2 < NT:
                 quantise(q // 2 + 2)
-            if q >= 0 and NHEAD + q // 4 < NT:
+            if NHEAD + q // 4 < NT:
                 widen(NHEAD + q // 4, D // 2 * (q // 2 % 2), D // 2 * (q // 2 % 2) + D // 2)
 
 
@@ -296,10 +299,11 @@ def tile_cmattention_pa_kernel(tc, x_bytes, x_scale, a, Wq_x, Wq_a, qx_scale, qa
                     turn_half(0, 1)
                     quantise(0)
 
-            for i in range(4, 8):
-                table_piece(0, i, on_vector=True)
             turn_half(1, 0)
             turn_half(1, 1)
+            for i in range(4, 8):
+                table_piece(0, i, on_vector=True)
+            quantise(1)
             for t in range(2, NHEAD):
                 widen(t)
 
@@ -357,8 +361,8 @@ def tile_cmattention_pa_kernel(tc, x_bytes, x_scale, a, Wq_x, Wq_a, qx_scale, qa
                     root(0)
                     turn_half(2, 0)
                 if q >= 0:
-                    if q // 8 + 1 < NBLK:
-                        table_piece(q // 8 + 1, q % 8)
+                    if q >= 1 and (q - 1) // 8 + 1 < NBLK:
+                        table_piece((q - 1) // 8 + 1, (q - 1) % 8)
                     if q + 1 < NQ:
                         clamp(q + 1)
                     if (q + 4 + q % 2) // 2 < NT:
@@ -379,9 +383,7 @@ def tile_cmattention_pa_kernel(tc, x_bytes, x_scale, a, Wq_x, Wq_a, qx_scale, qa
                             tx = (q + 5) // 2
                             nc.vector.tensor_copy(out=groupeds[tx][:, 0, :, :, :].bitcast(F32),
                                                   in_=xbanks[tx][:].rearrange("p g u r -> p g r u"))
-                if q == -2:
-                    prep_steps(q)
-                elif q >= 1 and q % 2 == 1:
+                if q >= 1 and q % 2 == 1:
                     prep_steps(q - 1)
                 if q >= 0:
                     product(q, prods[1], 1, HGRP - 1)

from contextlib import ExitStack

import concourse.mybir as mybir
from concourse.masks import make_identity

F32 = mybir.dt.float32
BF16 = mybir.dt.bfloat16
U32 = mybir.dt.uint32
U8 = mybir.dt.uint8
I32 = mybir.dt.int32
FP8 = mybir.dt.float8_e4m3fn
FP8X4 = mybir.dt.float8_e4m3fn_x4
ALU = mybir.AluOpType
ACT = mybir.ActivationFunctionType

B, N, D, H, DH = 4, 640, 1024, 16, 64
P = 128
NBLK = N // P
NPASS = D // 512
HGRP = 8
NT = B * NBLK
NQ = 2 * NT
NHEAD = 12
FLOPS = 2 * 2 * B * N * D * H * DH

TWO_PI = 6.283185307179586
C1 = 6.28125
C2 = TWO_PI - C1


def tile_cmattention_pa_kernel(tc, x_bytes, x_scale, a, Wq_x, Wq_a, qx_scale, qa_scale, out):
    nc = tc.nc
    with ExitStack() as ctx:
        const = ctx.enter_context(tc.tile_pool(name="const", bufs=1))
        ldpool = ctx.enter_context(tc.tile_pool(name="ldpool", bufs=2))
        prep = ctx.enter_context(tc.tile_pool(name="prep", bufs=2))
        tabs = ctx.enter_context(tc.tile_pool(name="tabs", bufs=2))
        tp = ctx.enter_context(tc.psum_pool(name="tp", bufs=2))
        mm = ctx.enter_context(tc.psum_pool(name="mm", bufs=6))

        W_in = (Wq_x, Wq_a)
        tiles = [(blk, b) for blk in range(NBLK) for b in range(B)]
        x8s = {}
        a_sbs = {}
        xbfs = {}
        groupeds = {}
        codes = {}
        banks = {}
        rs = {}
        sums = {}
        clamped = {}
        T = {}

        def load_x(blk):
            xt = ldpool.tile([P, B, D], U8, name="x8", tag="x8", bufs=NBLK)
            nc.sync.dma_start(out=xt[:], in_=x_bytes[:, blk * P:(blk + 1) * P, :].rearrange("b p k -> p b k"))
            x8s[blk] = xt

        def load_a(blk, b0, b1):
            if b0 == 0:
                at = ldpool.tile([P, B, D], BF16, name="a_sb", tag="a_sb")
                a_sbs[blk] = at
            nc.sync.dma_start(out=a_sbs[blk][:, b0:b1, :], in_=a[b0:b1, blk * P:(blk + 1) * P, :].rearrange("b p k -> p b k"))

        def load_blk(blk):
            load_x(blk)
            load_a(blk, 0, B)

        ident = const.tile([P, P], F32, name="ident")
        make_identity(nc, ident[:])
        tiny = const.tile([P, 1], F32, name="tiny")
        nc.vector.memset(tiny[:], 1e-24)
        warm0 = const.tile([P, 1], F32, name="warm0")
        nc.scalar.activation(out=warm0[:], in_=tiny[:], func=ACT.Sin)
        negtiny = const.tile([P, 1], F32, name="negtiny")
        nc.vector.memset(negtiny[:], -1e-24)
        xs_bc = const.tile([P, D], F32, name="xs_bc")
        identb = const.tile([P, P], BF16, name="identb")
        make_identity(nc, identb[:])
        NFN = 3
        csT = const.tile([P, NFN * NBLK, P], BF16, name="csT")
        gcol = const.tile([P, 2 * H], F32, name="gcol")
        Bg = [const.tile([P, H, DH], BF16, name="Bg%d" % v) for v in range(2)]
        wcodes = [const.tile([P, NPASS, H * DH], U32, name="wcodes%d" % s, align_bytes=64) for s in range(2)]
        wscl = [const.tile([P, NPASS, H * DH], U8, name="wscl%d" % s, align_bytes=64) for s in range(2)]

        def transpose_rows(bank, words):
            for g in range(NPASS):
                for u in range(2):
                    nc.tensor.transpose(bank[:, g, u, :], words[:, 256 * g + u:256 * (g + 1):2], ident[:])

        def table_piece(blk, i, on_vector=False):
            h0 = HGRP * (i // 4)
            tab = (i // 2) % 2
            e = i % 2
            fn = e if tab == 0 else 2 - 2 * e
            if (blk, tab) not in T:
                T[(blk, tab)] = tabs.tile([P, H, 2, DH], F32, name="T%d" % tab, tag="T%d" % tab)
            if on_vector:
                bank = mm.tile([P, 512], F32, name="mmbank", tag="mmbank")
            else:
                bank = tp.tile([P, 512], F32, name="tpbank", tag="tpbank")
            nc.tensor.matmul(out=bank[:], lhsT=csT[:, NFN * blk + fn, :],
                             rhs=Bg[tab][:, h0:h0 + HGRP, :].rearrange("p h j -> p (h j)"), start=True, stop=True)
            dst = T[(blk, tab)][:, h0:h0 + HGRP, e, :]
            src = bank[:].rearrange("p (h j) -> p h j", j=DH)
            if on_vector:
                nc.vector.tensor_copy(out=dst, in_=src)
            else:
                nc.scalar.copy(out=dst, in_=src)

        xbanks = {}

        def vcopy(t):
            return False

        def widen(t, k0=0, k1=D):
            blk, b = tiles[t]
            if k0 == 0:
                xbf = prep.tile([P, D], BF16, name="xbf", tag="xbf", bufs=NHEAD + 1)
                xbfs[t] = xbf
            nc.vector.tensor_tensor(out=xbfs[t][:, k0:k1], in0=x8s[blk][:, b, k0:k1].bitcast(FP8),
                                    in1=xs_bc[:, k0:k1], op=ALU.mult)

        def turn_half(t, s):
            blk, b = tiles[t]
            if s == 0:
                grouped = prep.tile([P, 2, NPASS, P, 4], BF16, name="grouped", tag="grouped", align_bytes=64)
                groupeds[t] = grouped
            src = xbfs[t][:].bitcast(F32) if s == 0 else a_sbs[blk][:, b, :].bitcast(F32)
            bank = tp.tile([P, NPASS, 2, P], F32, name="tpbank", tag="tpbank")
            transpose_rows(bank, src)
            if s == 0 and vcopy(t):
                xbanks[t] = bank
            else:
                nc.scalar.copy(out=groupeds[t][:, s, :, :, :].bitcast(F32), in_=bank[:].rearrange("p g u r -> p g r u"))
            if s == 1 and t % B == B - 1 and t // B + 2 < NBLK:
                load_a(t // B + 2, 0, B)

        def quantise(t):
            cd = prep.tile([P, 2, NPASS, P], U32, name="codes", tag="codes", bufs=3, align_bytes=64)
            sc = prep.tile([P, 2, NPASS, P], U8, name="scl", tag="scl", bufs=3, align_bytes=64)
            nc.vector.quantize_mx(
                out=cd[:].rearrange("p s g r -> p (s g r)").bitcast(FP8X4),
                scales=sc[:].rearrange("p s g r -> p (s g r)"),
                in_=groupeds[t][:].rearrange("p s g r j -> p (s g r j)"),
            )
            codes[t] = (cd, sc)

        def matmuls(q):
            t, hg = q // 2, q % 2
            cd, sc = codes[t]
            pair = []
            for s in range(2):
                ps = mm.tile([P, 512], F32, name="mmbank", tag="mmbank")
                for g in range(NPASS):
                    nc.tensor.matmul_mx(
                        out=ps[:],
                        lhsT=cd[:, s, g, :].bitcast(FP8X4),
                        lhsT_scale=sc[:, s, g, :],
                        rhs=wcodes[s][:, g, hg * 512:(hg + 1) * 512].bitcast(FP8X4),
                        rhs_scale=wscl[s][:, g, hg * 512:(hg + 1) * 512],
                        start=(g == 0),
                        stop=(g == NPASS - 1),
                    )
                pair.append(ps)
            banks[q] = pair

        def prep_steps(q):
            if q // 2 + 2 < NT:
                quantise(q // 2 + 2)
            if NHEAD + q // 4 < NT:
                widen(NHEAD + q // 4, D // 2 * (q // 2 % 2), D // 2 * (q // 2 % 2) + D // 2)


        sq = ctx.enter_context(tc.tile_pool(name="sq", bufs=3))

        with tc.tile_pool(name="head", bufs=1) as head:
            graw = head.tile([P, P], BF16, name="graw")
            nc.vector.memset(graw[:], 0.0)
            for s in range(2):
                for e in range(2):
                    nc.sync.dma_start(out=graw[s * H:(s + 1) * H, e * DH:(e + 1) * DH],
                                      in_=(qx_scale, qa_scale)[s].rearrange("h o j -> h (o j)"))
            sraw = head.tile([P, P], F32, name="sraw")
            nc.vector.memset(sraw[:], 0.0)
            nc.sync.dma_start(out=sraw[0:D // P, :], in_=x_scale.rearrange("o q (c p) -> (o q c) p", p=P))
            load_x(0)
            wraw = {}

            def load_w(s, half):
                t = head.tile([P, 4, D], BF16, name="wraw%d%d" % (s, half))
                for c in range(2):
                    nc.sync.dma_start(
                        out=t[:, 2 * c:2 * c + 2, :],
                        in_=W_in[s][half * 512 + c * 256:half * 512 + (c + 1) * 256, :].rearrange("(r p) k -> p r k", p=P),
                    )
                wraw[(s, half)] = t

            load_w(0, 0)
            load_w(1, 0)
            load_a(0, 0, 2)
            load_w(0, 1)
            load_w(1, 1)
            load_a(0, 2, B)
            load_x(1)
            load_x(2)
            load_a(1, 0, B)
            load_x(3)
            load_x(4)

            gf = head.tile([P, P], F32, name="gf")
            nc.vector.tensor_copy(out=gf[:], in_=graw[:])
            gbank = tp.tile([P, 512], F32, name="tpbank", tag="tpbank")
            nc.tensor.transpose(gbank[:, 0:P], gf[:], ident[:])
            nc.tensor.transpose(gbank[:, P:2 * P], sraw[:], ident[:])
            scol = head.tile([P, D // P], F32, name="scol")
            nc.scalar.copy(out=scol[:], in_=gbank[:, P:P + D // P])
            nc.scalar.copy(out=gcol[:], in_=gbank[:, 0:2 * H])
            id2 = head.tile([P, DH], BF16, name="id2")
            nc.vector.tensor_tensor(out=id2[:], in0=ident[:, 0:DH], in1=ident[:, DH:P], op=ALU.add)
            nc.vector.tensor_tensor(out=Bg[0][:], in0=id2[:].unsqueeze(1).to_broadcast([P, H, DH]),
                                    in1=gcol[:, 0:H].unsqueeze(2).to_broadcast([P, H, DH]), op=ALU.mult)
            for h in range(H):
                nc.scalar.activation(out=Bg[1][:, h, :], in_=id2[:], func=ACT.Copy, scale=gcol[:, H + h:H + h + 1])

            for c2 in range(2):
                bank = tp.tile([P, 4, P], F32, name="tpbank", tag="tpbank")
                for k in range(4):
                    nc.tensor.transpose(bank[:, k, :], scol[:, 4 * c2 + k:4 * c2 + k + 1].to_broadcast([P, P]), ident[:])
                nc.scalar.copy(out=xs_bc[:, c2 * 512:(c2 + 1) * 512], in_=bank[:].rearrange("p k n -> p (k n)"))

            freq = head.tile([P, DH], F32, name="freq")
            nc.vector.memset(freq[:], 1.0)
            for bit in range(6):
                c = 2 ** bit
                view = freq[:].rearrange("p (a two c) -> p a two c", two=2, c=c)[:, :, 1, :]
                nc.vector.tensor_scalar_mul(out=view, in0=view, scalar1=10000.0 ** (-c / 64.0))
            n_i = head.tile([P, NBLK], I32, name="n_i")
            nc.gpsimd.iota(n_i[:], pattern=[[P, NBLK]], base=0, channel_multiplier=1)
            theta = head.tile([P, NBLK, DH], F32, name="theta")
            nc.vector.tensor_tensor(out=theta[:], in0=n_i[:].unsqueeze(2).to_broadcast([P, NBLK, DH]),
                                    in1=freq[:].unsqueeze(1).to_broadcast([P, NBLK, DH]), op=ALU.mult)
            k_i = head.tile([P, NBLK, DH], I32, name="k_i")
            nc.vector.tensor_scalar_mul(out=k_i[:], in0=theta[:], scalar1=1.0 / TWO_PI)
            red1 = head.tile([P, NBLK, DH], F32, name="red1")
            nc.vector.scalar_tensor_tensor(out=red1[:], in0=k_i[:], scalar=-C1, in1=theta[:],
                                           op0=ALU.mult, op1=ALU.add)
            red = head.tile([P, NBLK, DH], F32, name="red")
            nc.vector.scalar_tensor_tensor(out=red[:], in0=k_i[:], scalar=-C2, in1=red1[:],
                                           op0=ALU.mult, op1=ALU.add)
            trig = head.tile([P, NBLK, 2, DH], F32, name="trig")
            s2 = head.tile([P, NBLK, DH], F32, name="s2")
            nc.scalar.activation(out=s2[:], in_=red[:], func=ACT.Sin, scale=0.5)
            nc.scalar.activation(out=trig[:, :, 1, :], in_=red[:], func=ACT.Sin)
            warm = head.tile([P, 1], F32, name="warm")
            nc.scalar.activation(out=warm[:], in_=trig[:, 0, 1, 0:1], func=ACT.Abs_reciprocal_sqrt, bias=tiny[:, 0:1])
            q2 = head.tile([P, NBLK, DH], F32, name="q2")
            nc.vector.tensor_tensor(out=q2[:], in0=s2[:], in1=s2[:], op=ALU.mult)
            nc.vector.tensor_scalar(out=trig[:, :, 0, :], in0=q2[:], scalar1=-2.0, scalar2=1.0,
                                    op0=ALU.mult, op1=ALU.add)
            hl = head.tile([P, NBLK, NFN, 2, DH], BF16, name="hl")
            nc.vector.tensor_copy(out=hl[:, :, 0:2, 0, :], in_=trig[:])
            nc.vector.tensor_tensor(out=hl[:, :, 0:2, 1, :], in0=trig[:], in1=hl[:, :, 0:2, 0, :], op=ALU.subtract)
            nc.vector.tensor_scalar_mul(out=hl[:, :, 2, :, :], in0=hl[:, :, 1, :, :], scalar1=-1.0)

            for half in range(2):
                for s in range(2):
                    gww = head.tile([P, NPASS, 512, 4], BF16, name="gww", tag="gww", bufs=2, align_bytes=64)
                    for rr in range(4):
                        bank = mm.tile([P, NPASS, 2, P], F32, name="mmbank", tag="mmbank")
                        transpose_rows(bank, wraw[(s, half)][:, rr, :].bitcast(F32))
                        dst = gww[:, :, rr * P:(rr + 1) * P, :].bitcast(F32)
                        src = bank[:].rearrange("p g u r -> p g r u")
                        if rr < 0:
                            nc.vector.tensor_copy(out=dst, in_=src)
                        else:
                            nc.scalar.copy(out=dst, in_=src)
                    for g in range(NPASS):
                        nc.vector.quantize_mx(
                            out=wcodes[s][:, g, half * 512:(half + 1) * 512].bitcast(FP8X4),
                            scales=wscl[s][:, g, half * 512:(half + 1) * 512],
                            in_=gww[:, g, :, :].rearrange("p c j -> p (c j)"),
                        )
                if half == 0:
                    for i0 in range(0, NFN * NBLK, 4):
                        cnt = min(4, NFN * NBLK - i0)
                        bank = tp.tile([P, 4, P], BF16, name="tpbank", tag="tpbank")
                        for k in range(cnt):
                            i = i0 + k
                            nc.tensor.transpose(bank[:, k, :], hl[:, i // NFN, i % NFN, :, :].rearrange("p t j -> p (t j)"),
                                                identb[:])
                        nc.scalar.copy(out=csT[:, i0:i0 + cnt, :], in_=bank[:, 0:cnt, :])
                    for i in range(4):
                        table_piece(0, i)
                    for t in range(2):
                        widen(t)
                    turn_half(0, 0)
                    turn_half(0, 1)
                    quantise(0)

            turn_half(1, 0)
            turn_half(1, 1)
            for i in range(4, 8):
                table_piece(0, i, on_vector=True)
            quantise(1)
            for t in range(2, NHEAD):
                widen(t)

        epi = ctx.enter_context(tc.tile_pool(name="epi", bufs=3))

        def squares(q):
            junk = sq.tile([P, 2 * HGRP, DH], BF16, name="junk", tag="junk", bufs=2)
            ss = sq.tile([P, 2 * HGRP], F32, name="ss", tag="ss")
            for s in range(2):
                for hh in range(HGRP):
                    i = s * HGRP + hh
                    nc.scalar.activation(out=junk[:, i, :], in_=banks[q][s][:, DH * hh:DH * (hh + 1)],
                                         func=ACT.Square, accum_out=ss[:, i:i + 1])
            sums[q] = ss

        def clamp(q):
            fl = sq.tile([P, 2 * HGRP], F32, name="fl", tag="fl")
            nc.scalar.activation(out=fl[:], in_=sums[q][:], func=ACT.Relu, bias=negtiny[:, 0:1])
            clamped[q] = fl

        def root(q):
            r = sq.tile([P, 2 * HGRP], F32, name="r", tag="r")
            nc.scalar.activation(out=r[:], in_=clamped[q][:], func=ACT.Abs_reciprocal_sqrt, bias=tiny[:, 0:1])
            rs[q] = r

        def product(q, prod, s, hh):
            t, hg = q // 2, q % 2
            blk = tiles[t][0]
            h = hg * HGRP + hh
            nc.vector.scalar_tensor_tensor(
                out=prod[:, h, :, :],
                in0=banks[q][s][:, DH * hh:DH * (hh + 1)].unsqueeze(1).to_broadcast([P, 2, DH]),
                scalar=rs[q][:, s * HGRP + hh:s * HGRP + hh + 1],
                in1=T[(blk, s)][:, h, :, :],
                op0=ALU.mult,
                op1=ALU.mult,
            )

        def store(t, o, h0, h1):
            blk, b = tiles[t]
            nc.sync.dma_start(
                out=out[b, h0:h1, blk * P:(blk + 1) * P, :].rearrange("h n d -> n h d"),
                in_=o[:, h0:h1, :, :].rearrange("p h e j -> p h (e j)"),
            )

        with tc.manual_schedule(engines={mybir.EngineType.DVE, mybir.EngineType.PE, mybir.EngineType.Activation}):
            prods = []
            for q in range(-2, NQ):
                if q < 0:
                    matmuls(q + 2)
                if 0 <= q + 1 < NQ:
                    squares(q + 1)
                if q == -1:
                    clamp(0)
                    root(0)
                    turn_half(2, 0)
                if q >= 0:
                    if q >= 1 and (q - 1) // 8 + 1 < NBLK:
                        table_piece((q - 1) // 8 + 1, (q - 1) % 8)
                    if q + 1 < NQ:
                        clamp(q + 1)
                    if (q + 4 + q % 2) // 2 < NT:
                        turn_half((q + 4 + q % 2) // 2, (q + 1) % 2)
                    if q + 1 < NQ:
                        root(q + 1)
                    if q + 2 < NQ:
                        matmuls(q + 2)
                if q >= 0:
                    if q % 2 == 0:
                        prods = []
                        for s in range(2):
                            prod = epi.tile([P, H, 2, DH], F32, name="prod%d" % s, tag="prod%d" % s, bufs=2)
                            prods.append(prod)
                    for i in range(2 * HGRP - 1):
                        product(q, prods[i % 2], i % 2, i // 2)
                        if i == 11 and (q + 5) // 2 in xbanks and q % 2 == 1:
                            tx = (q + 5) // 2
                            nc.vector.tensor_copy(out=groupeds[tx][:, 0, :, :, :].bitcast(F32),
                                                  in_=xbanks[tx][:].rearrange("p g u r -> p g r u"))
                if q >= 1 and q % 2 == 1:
                    prep_steps(q - 1)
                if q >= 0:
                    product(q, prods[1], 1, HGRP - 1)
                    if q % 2 == 1:
                        t = q // 2
                        o = epi.tile([P, H, 2, DH], F32, name="o", tag="o", bufs=2)
                        if t < NT - 1:
                            nc.gpsimd.tensor_tensor(out=o[:], in0=prods[0][:], in1=prods[1][:], op=ALU.add)
                            store(t, o, 0, H)
                        else:
                            for h0 in range(0, H, 4):
                                nc.vector.tensor_tensor(out=o[:, h0:h0 + 4, :, :], in0=prods[0][:, h0:h0 + 4, :, :],
                                                        in1=prods[1][:, h0:h0 + 4, :, :], op=ALU.add)
                                store(t, o, h0, h0 + 4)
